import numpy as np
import ml_dtypes


def mxq(x, axis, fmt="e4m3"):
    dtype, down = {"e4m3": (ml_dtypes.float8_e4m3fn, 7), "e5m2": (ml_dtypes.float8_e5m2, 14)}[fmt]
    v = np.moveaxis(np.asarray(x, np.float32).astype(ml_dtypes.bfloat16).astype(np.float64), axis, -1)
    blocks = v.reshape(v.shape[:-1] + (-1, 32))
    amax = np.abs(blocks).max(-1, keepdims=True)
    byte = np.maximum(np.where(amax > 0, np.frexp(amax)[1] - 1 + 127, 0) - down, 1)
    scale = np.exp2(byte - 127.0)
    codes = (blocks / scale).astype(np.float32).astype(dtype).astype(np.float64)
    return np.moveaxis((codes * scale).reshape(v.shape), -1, axis)


WIDE = False


def mx_kscale(k):
    if not WIDE:
        return np.ones(k)
    levels = np.array([10, -10, 5, -5, 0])
    if k % 512:
        return np.exp2(np.random.permutation(np.resize(levels, k // 32))).repeat(32)
    a = np.empty((k // 512, 16))
    for p in range(k // 512):
        a[p, :8] = np.random.permutation(np.resize(levels, 8))
        for g in range(8):
            far = levels[np.abs(levels - a[p, g]) >= 10]
            a[p, g + 8] = far[np.random.randint(len(far))]
    return np.exp2(a.ravel()).repeat(32)


BF16 = ml_dtypes.bfloat16


def bf(x):
    return np.asarray(x, np.float32).astype(BF16)


def f64(x):
    return np.asarray(x).astype(np.float64)


B, MI, MO, NL = 128, 1536, 1536, 4
IR_DIMS = tuple(2 * l + 1 for l in range(NL))
FLAT_IN = MI * sum(IR_DIMS)


def setup_inputs():
    s = mx_kscale(MI)
    sx = np.concatenate([np.repeat(s, d) for d in IR_DIMS])
    inp = {"x": bf(np.random.standard_normal((B, FLAT_IN)) * sx)}
    for l in range(NL):
        inp["W%d" % l] = bf(np.random.standard_normal((MO, MI)) / np.sqrt(MI) / s[None, :])
    inp["bias"] = bf(np.random.standard_normal(MO))
    return inp


def reference(x, W0, W1, W2, W3, bias):
    x = f64(x)
    outs = []
    start = 0
    for d, W in zip(IR_DIMS, (W0, W1, W2, W3)):
        seg = x[:, start:start + MI * d].reshape(B, MI, d)
        rows = seg.transpose(0, 2, 1).reshape(B * d, MI)
        y = mxq(rows, 1, "e4m3") @ mxq(f64(W).T, 0, "e4m3")
        outs.append(y.reshape(B, d, MO).transpose(0, 2, 1).reshape(B, MO * d))
        start += MI * d
    outs[0] = outs[0] + f64(bias)
    return np.concatenate(outs, axis=1)

@@ -1,0 +1,198 @@
+from contextlib import ExitStack
+
+import concourse.mybir as mybir
+from concourse.masks import make_identity
+
+F32 = mybir.dt.float32
+BF16 = mybir.dt.bfloat16
+U32 = mybir.dt.uint32
+U8 = mybir.dt.uint8
+FP8X4 = mybir.dt.float8_e4m3fn_x4
+
+P = 128
+CHANNELS = 1536
+IRREP_DIMS = (1, 3, 5, 7)
+SEGMENT_START = (0, 1536, 6144, 13824)
+K_PASS = 512
+THIRDS = CHANNELS // K_PASS
+HALVES = 2
+PASS_WORDS = K_PASS // 2
+CHUNK = 512
+ROWS = CHUNK // P
+LINE = 4
+
+SEGMENT_ORDER = (1, 2, 3, 0)
+
+X_LOAD_LEAD = 6
+X_SPLIT_LEAD = 5
+X_PACK_LEAD = 3
+W_LOAD_LEAD = 4
+W_PACK_LEAD = 2
+
+FLOPS = 2 * P * sum(IRREP_DIMS) * CHANNELS * CHANNELS
+
+
+def channels_to_partitions(nc, banks, identity, rows, grouped, drain):
+    bank = banks.tile([P, 2, HALVES, P], F32, tag="bank")
+    for s, words in enumerate(rows):
+        for u in range(HALVES):
+            nc.tensor.transpose(bank[:, s, u, :], words[:, u:PASS_WORDS:HALVES], identity)
+    drain(out=grouped, in_=bank[:, : len(rows)].rearrange("p s u r -> p s r u"))
+
+
+def tile_so3_linear_pa_kernel(tc, x, W0, W1, W2, W3, bias, out):
+    nc = tc.nc
+    weights = (W0, W1, W2, W3)
+    steps = [(l, third) for l in SEGMENT_ORDER for third in range(THIRDS)]
+
+    with ExitStack() as ctx:
+        keep = ctx.enter_context(tc.tile_pool(name="keep", bufs=1))
+        stream = ctx.enter_context(tc.tile_pool(name="stream", bufs=2))
+        banks = ctx.enter_context(tc.psum_pool(name="banks", bufs=8))
+        ctx.enter_context(tc.manual_schedule())
+
+        identity = keep.tile([P, P], F32)
+        make_identity(nc, identity[:])
+        bias_rows = keep.tile([P, CHANNELS], BF16)
+        x_codes = {}
+        x_scales = {}
+        for l, d in enumerate(IRREP_DIMS):
+            codes = keep.tile([P, THIRDS, d * P], U32, name="x_codes%d" % l, align_bytes=64)
+            scales = keep.tile([P, THIRDS, d * P], U8, name="x_scales%d" % l, align_bytes=64)
+            x_codes[l] = codes
+            x_scales[l] = scales
+        x_raw = {}
+        x_split = {}
+        w_raw = {}
+        w_packed = {}
+
+        def load_x(q):
+            l, g = steps[q]
+            d = IRREP_DIMS[l]
+            first = SEGMENT_START[l] + g * K_PASS * d
+            raw = stream.tile([P, K_PASS * d], BF16, name="x_raw", bufs=4)
+            nc.sync.dma_start(out=raw[:], in_=x[:, first : first + K_PASS * d])
+            x_raw[q] = raw
+
+        def split_x(q):
+            d = IRREP_DIMS[steps[q][0]]
+            split = stream.tile([P, d * K_PASS], BF16, name="x_split", bufs=3)
+            nc.vector.tensor_copy(
+                out=split[:].rearrange("p (i m) -> p i m", i=d),
+                in_=x_raw[q][:].rearrange("p (m i) -> p i m", i=d),
+            )
+            x_split[q] = split
+
+        def pack_x(q):
+            l, g = steps[q]
+            d = IRREP_DIMS[l]
+            words = x_split[q][:].bitcast(F32)
+            grouped = stream.tile([P, d * K_PASS], BF16, name="x_grouped", align_bytes=64)
+            grouped_words = grouped[:].bitcast(F32)
+            pairs = [(i, min(2, d - i)) for i in range(0, d, 2)]
+            for i, n in pairs:
+                channels_to_partitions(
+                    nc,
+                    banks,
+                    identity[:],
+                    [words[:, (i + s) * PASS_WORDS : (i + s + 1) * PASS_WORDS] for s in range(n)],
+                    grouped_words[:, i * PASS_WORDS : (i + n) * PASS_WORDS].rearrange(
+                        "p (s r u) -> p s r u", s=n, u=HALVES
+                    ),
+                    nc.vector.tensor_copy,
+                )
+            for i, n in pairs:
+                nc.vector.quantize_mx(
+                    out=x_codes[l][:, g, i * P : (i + n) * P].bitcast(FP8X4),
+                    scales=x_scales[l][:, g, i * P : (i + n) * P],
+                    in_=grouped[:, i * K_PASS : (i + n) * K_PASS],
+                )
+
+        def load_w(q):
+            l, c = steps[q]
+            raw = stream.tile([P, ROWS * CHANNELS], BF16, name="w_raw", bufs=3)
+            nc.sync.dma_start(
+                out=raw[:],
+                in_=weights[l][c * CHUNK : (c + 1) * CHUNK, :].rearrange("(j r) m -> j (r m)", r=ROWS),
+            )
+            w_raw[q] = raw
+
+        def pack_w(q):
+            words = w_raw[q][:].bitcast(F32)
+            row_words = CHANNELS // 2
+            grouped = stream.tile([P, THIRDS * CHUNK * 4], BF16, name="w_grouped", align_bytes=64)
+            grouped_words = grouped[:].bitcast(F32)
+            codes = stream.tile([P, THIRDS, CHUNK], U32, name="w_codes", bufs=3, align_bytes=64)
+            scales = stream.tile([P, THIRDS, CHUNK], U8, name="w_scales", bufs=3, align_bytes=64)
+            for g in range(THIRDS):
+                for r in range(0, ROWS, 2):
+                    first = (g * CHUNK + r * P) * HALVES
+                    channels_to_partitions(
+                        nc,
+                        banks,
+                        identity[:],
+                        [
+                            words[:, (r + s) * row_words + g * PASS_WORDS : (r + s) * row_words + (g + 1) * PASS_WORDS]
+                            for s in range(2)
+                        ],
+                        grouped_words[:, first : first + 2 * P * HALVES].rearrange(
+                            "p (s r u) -> p s r u", s=2, u=HALVES
+                        ),
+                        nc.scalar.copy,
+                    )
+                nc.vector.quantize_mx(
+                    out=codes[:, g, :].bitcast(FP8X4),
+                    scales=scales[:, g, :],
+                    in_=grouped[:, g * CHUNK * 4 : (g + 1) * CHUNK * 4],
+                )
+            w_packed[q] = (codes, scales)
+
+        def multiply(q):
+            l, c = steps[q]
+            d = IRREP_DIMS[l]
+            codes, scales = w_packed[q]
+            result = stream.tile([P, CHUNK * d], F32, name="result", bufs=3)
+            lines = result[:].rearrange("p (j k s) -> p j k s", k=d, s=LINE)
+            for k in range(d):
+                acc = banks.tile([P, LINE, P], F32, tag="bank")
+                for s in range(LINE):
+                    r, i = divmod(LINE * k + s, d)
+                    for g in range(THIRDS):
+                        nc.tensor.matmul_mx(
+                            out=acc[:, s, :],
+                            lhsT=x_codes[l][:, g, i * P : (i + 1) * P].bitcast(FP8X4),
+                            lhsT_scale=x_scales[l][:, g, i * P : (i + 1) * P],
+                            rhs=codes[:, g, r * P : (r + 1) * P].bitcast(FP8X4),
+                            rhs_scale=scales[:, g, r * P : (r + 1) * P],
+                            start=(g == 0),
+                            stop=(g == THIRDS - 1),
+                        )
+                by_line = acc[:].rearrange("p s j -> p j s")
+                if l == 0:
+                    nc.vector.tensor_tensor(
+                        out=lines[:, :, k, :],
+                        in0=by_line,
+                        in1=bias_rows[:, c * CHUNK : (c + 1) * CHUNK].rearrange("p (j s) -> p j s", s=LINE),
+                        op=mybir.AluOpType.add,
+                    )
+                else:
+                    nc.scalar.copy(out=lines[:, :, k, :], in_=by_line)
+            first = SEGMENT_START[l] + c * CHUNK * d
+            nc.scalar.dma_start(out=out[:, first : first + CHUNK * d], in_=result[:])
+
+        last = len(steps)
+        for now in range(-X_LOAD_LEAD, last):
+            if 0 <= now + W_LOAD_LEAD < last:
+                load_w(now + W_LOAD_LEAD)
+            if now + X_LOAD_LEAD < last:
+                load_x(now + X_LOAD_LEAD)
+            if now + X_LOAD_LEAD == last:
+                nc.sync.dma_start(out=bias_rows[:], in_=bias.partition_broadcast(P))
+            if 0 <= now + W_PACK_LEAD < last:
+                pack_w(now + W_PACK_LEAD)
+            if 0 <= now + X_PACK_LEAD < last:
+                pack_x(now + X_PACK_LEAD)
+            if 0 <= now + X_SPLIT_LEAD < last:
+                split_x(now + X_SPLIT_LEAD)
+            if 0 <= now:
+                multiply(now)

@@ -16,6 +16,8 @@ SEGMENT_START = (0, 1536, 6144, 13824)
 K_PASS = 512
 THIRDS = CHANNELS // K_PASS
 HALVES = 2
+RUN = 16
+BLOCKS = K_PASS // (HALVES * RUN)
 PASS_WORDS = K_PASS // 2
 CHUNK = 512
 ROWS = CHUNK // P
@@ -25,19 +27,14 @@ SEGMENT_ORDER = (1, 2, 3, 0)
 
 X_LOAD_LEAD = 6
 X_SPLIT_LEAD = 5
-X_PACK_LEAD = 3
+X_TURN_LEAD = 4
+X_QUANT_LEAD = 3
 W_LOAD_LEAD = 4
-W_PACK_LEAD = 2
+W_SORT_LEAD = 3
+W_TURN_LEAD = 2
+W_QUANT_LEAD = 1
 
 FLOPS = 2 * P * sum(IRREP_DIMS) * CHANNELS * CHANNELS
-
-
-def channels_to_partitions(nc, banks, identity, rows, grouped, drain):
-    bank = banks.tile([P, 2, HALVES, P], F32, tag="bank")
-    for s, words in enumerate(rows):
-        for u in range(HALVES):
-            nc.tensor.transpose(bank[:, s, u, :], words[:, u:PASS_WORDS:HALVES], identity)
-    drain(out=grouped, in_=bank[:, : len(rows)].rearrange("p s u r -> p s r u"))
 
 
 def tile_so3_linear_pa_kernel(tc, x, W0, W1, W2, W3, bias, out):
@@ -63,50 +60,68 @@ def tile_so3_linear_pa_kernel(tc, x, W0, W1, W2, W3, bias, out):
             x_scales[l] = scales
         x_raw = {}
         x_split = {}
+        x_grouped = {}
         w_raw = {}
+        w_sorted = {}
+        w_grouped = {}
         w_packed = {}
+
+        def turn(words_of, columns, grouped, drain):
+            bank = banks.tile([P, 2, HALVES, P], F32, tag="bank")
+            for s in range(columns):
+                for u in range(HALVES):
+                    nc.tensor.transpose(bank[:, s, u, :], words_of(s, u), identity[:])
+            drain(out=grouped, in_=bank[:, :columns].rearrange("p s u r -> p s r u"))
 
         def load_x(q):
             l, g = steps[q]
             d = IRREP_DIMS[l]
             first = SEGMENT_START[l] + g * K_PASS * d
-            raw = stream.tile([P, K_PASS * d], BF16, name="x_raw", bufs=4)
+            raw = stream.tile([P, K_PASS * d], BF16, name="x_raw", bufs=3)
             nc.sync.dma_start(out=raw[:], in_=x[:, first : first + K_PASS * d])
             x_raw[q] = raw
 
         def split_x(q):
             d = IRREP_DIMS[steps[q][0]]
-            split = stream.tile([P, d * K_PASS], BF16, name="x_split", bufs=3)
-            nc.vector.tensor_copy(
-                out=split[:].rearrange("p (i m) -> p i m", i=d),
-                in_=x_raw[q][:].rearrange("p (m i) -> p i m", i=d),
-            )
+            split = stream.tile([P, d, K_PASS], BF16, name="x_split", bufs=2)
+            by_component = x_raw[q][:].rearrange("p (c u v i) -> p c u v i", c=BLOCKS, u=HALVES, i=d)
+            parts = -(-d // 4)
+            for k in range(parts):
+                i0, i1 = k * d // parts, (k + 1) * d // parts
+                nc.vector.tensor_copy(
+                    out=split[:, i0:i1, :].rearrange("p i (u c v) -> p c u v i", u=HALVES, c=BLOCKS),
+                    in_=by_component[:, :, :, :, i0:i1],
+                )
             x_split[q] = split
 
-        def pack_x(q):
-            l, g = steps[q]
-            d = IRREP_DIMS[l]
-            words = x_split[q][:].bitcast(F32)
+        def turn_x(q):
+            d = IRREP_DIMS[steps[q][0]]
+            words = x_split[q][:].rearrange("p i m -> p (i m)").bitcast(F32)
             grouped = stream.tile([P, d * K_PASS], BF16, name="x_grouped", align_bytes=64)
             grouped_words = grouped[:].bitcast(F32)
-            pairs = [(i, min(2, d - i)) for i in range(0, d, 2)]
-            for i, n in pairs:
-                channels_to_partitions(
-                    nc,
-                    banks,
-                    identity[:],
-                    [words[:, (i + s) * PASS_WORDS : (i + s + 1) * PASS_WORDS] for s in range(n)],
+            for i in range(0, d, 2):
+                n = min(2, d - i)
+                turn(
+                    lambda s, u: words[:, (i + s) * PASS_WORDS + u * P : (i + s) * PASS_WORDS + (u + 1) * P],
+                    n,
                     grouped_words[:, i * PASS_WORDS : (i + n) * PASS_WORDS].rearrange(
                         "p (s r u) -> p s r u", s=n, u=HALVES
                     ),
                     nc.vector.tensor_copy,
                 )
-            for i, n in pairs:
-                nc.vector.quantize_mx(
-                    out=x_codes[l][:, g, i * P : (i + n) * P].bitcast(FP8X4),
-                    scales=x_scales[l][:, g, i * P : (i + n) * P],
-                    in_=grouped[:, i * K_PASS : (i + n) * K_PASS],
-                )
+            x_grouped[q] = grouped
+
+        def quantize_x(q):
+            l, g = steps[q]
+            d = IRREP_DIMS[l]
+            for i in range(0, d, 4):
+                n = min(4, d - i)
+                for a, b in ((i, i + n),) if n != 3 else ((i, i + 2), (i + 2, i + 3)):
+                    nc.vector.quantize_mx(
+                        out=x_codes[l][:, g, a * P : b * P].bitcast(FP8X4),
+                        scales=x_scales[l][:, g, a * P : b * P],
+                        in_=x_grouped[q][:, a * K_PASS : b * K_PASS],
+                    )
 
         def load_w(q):
             l, c = steps[q]
@@ -117,33 +132,39 @@ def tile_so3_linear_pa_kernel(tc, x, W0, W1, W2, W3, bias, out):
             )
             w_raw[q] = raw
 
-        def pack_w(q):
-            words = w_raw[q][:].bitcast(F32)
-            row_words = CHANNELS // 2
+        def sort_w(q):
+            result = stream.tile([P, ROWS * THIRDS, HALVES, P], F32, name="w_sorted")
+            nc.vector.tensor_copy(
+                out=result[:].rearrange("p t u (c v) -> p (t u) c v", v=RUN // 2),
+                in_=w_raw[q][:].bitcast(F32).rearrange("p (t c u v) -> p t u c v", t=ROWS * THIRDS, u=HALVES, v=RUN // 2),
+            )
+            w_sorted[q] = result
+
+        def turn_w(q):
+            words = w_sorted[q]
             grouped = stream.tile([P, THIRDS * CHUNK * 4], BF16, name="w_grouped", align_bytes=64)
             grouped_words = grouped[:].bitcast(F32)
-            codes = stream.tile([P, THIRDS, CHUNK], U32, name="w_codes", bufs=3, align_bytes=64)
-            scales = stream.tile([P, THIRDS, CHUNK], U8, name="w_scales", bufs=3, align_bytes=64)
             for g in range(THIRDS):
                 for r in range(0, ROWS, 2):
                     first = (g * CHUNK + r * P) * HALVES
-                    channels_to_partitions(
-                        nc,
-                        banks,
-                        identity[:],
-                        [
-                            words[:, (r + s) * row_words + g * PASS_WORDS : (r + s) * row_words + (g + 1) * PASS_WORDS]
-                            for s in range(2)
-                        ],
+                    turn(
+                        lambda s, u: words[:, (r + s) * THIRDS + g, u, :],
+                        2,
                         grouped_words[:, first : first + 2 * P * HALVES].rearrange(
                             "p (s r u) -> p s r u", s=2, u=HALVES
                         ),
                         nc.scalar.copy,
                     )
+            w_grouped[q] = grouped
+
+        def quantize_w(q):
+            codes = stream.tile([P, THIRDS, CHUNK], U32, name="w_codes", bufs=3, align_bytes=64)
+            scales = stream.tile([P, THIRDS, CHUNK], U8, name="w_scales", bufs=3, align_bytes=64)
+            for g in range(THIRDS):
                 nc.vector.quantize_mx(
                     out=codes[:, g, :].bitcast(FP8X4),
                     scales=scales[:, g, :],
-                    in_=grouped[:, g * CHUNK * 4 : (g + 1) * CHUNK * 4],
+                    in_=w_grouped[q][:, g * CHUNK * 4 : (g + 1) * CHUNK * 4],
                 )
             w_packed[q] = (codes, scales)
 
@@ -151,7 +172,7 @@ def tile_so3_linear_pa_kernel(tc, x, W0, W1, W2, W3, bias, out):
             l, c = steps[q]
             d = IRREP_DIMS[l]
             codes, scales = w_packed[q]
-            result = stream.tile([P, CHUNK * d], F32, name="result", bufs=3)
+            result = stream.tile([P, CHUNK * d], F32, name="result")
             lines = result[:].rearrange("p (j k s) -> p j k s", k=d, s=LINE)
             for k in range(d):
                 acc = banks.tile([P, LINE, P], F32, tag="bank")
@@ -181,18 +202,20 @@ def tile_so3_linear_pa_kernel(tc, x, W0, W1, W2, W3, bias, out):
             nc.scalar.dma_start(out=out[:, first : first + CHUNK * d], in_=result[:])
 
         last = len(steps)
+
+        def at(stage, q):
+            if 0 <= q < last:
+                stage(q)
+
         for now in range(-X_LOAD_LEAD, last):
-            if 0 <= now + W_LOAD_LEAD < last:
-                load_w(now + W_LOAD_LEAD)
-            if now + X_LOAD_LEAD < last:
-                load_x(now + X_LOAD_LEAD)
+            at(load_w, now + W_LOAD_LEAD)
+            at(load_x, now + X_LOAD_LEAD)
             if now + X_LOAD_LEAD == last:
                 nc.sync.dma_start(out=bias_rows[:], in_=bias.partition_broadcast(P))
-            if 0 <= now + W_PACK_LEAD < last:
-                pack_w(now + W_PACK_LEAD)
-            if 0 <= now + X_PACK_LEAD < last:
-                pack_x(now + X_PACK_LEAD)
-            if 0 <= now + X_SPLIT_LEAD < last:
-                split_x(now + X_SPLIT_LEAD)
-            if 0 <= now:
-                multiply(now)
+            at(sort_w, now + W_SORT_LEAD)
+            at(turn_w, now + W_TURN_LEAD)
+            at(turn_x, now + X_TURN_LEAD)
+            at(quantize_w, now + W_QUANT_LEAD)
+            at(quantize_x, now + X_QUANT_LEAD)
+            at(split_x, now + X_SPLIT_LEAD)
+            at(multiply, now)

@@ -25,14 +25,14 @@ LINE = 4
 
 SEGMENT_ORDER = (1, 2, 3, 0)
 
-X_LOAD_LEAD = 6
-X_SPLIT_LEAD = 5
-X_TURN_LEAD = 4
-X_QUANT_LEAD = 3
-W_LOAD_LEAD = 4
-W_SORT_LEAD = 3
-W_TURN_LEAD = 2
-W_QUANT_LEAD = 1
+W_LOAD = 6
+W_SORT = 3
+W_TURN = 2
+W_QUANT = 1
+X_LOAD = 10
+X_SPLIT = 8
+X_TURN = 7
+X_QUANT = 5
 
 FLOPS = 2 * P * sum(IRREP_DIMS) * CHANNELS * CHANNELS
 
@@ -40,7 +40,8 @@ FLOPS = 2 * P * sum(IRREP_DIMS) * CHANNELS * CHANNELS
 def tile_so3_linear_pa_kernel(tc, x, W0, W1, W2, W3, bias, out):
     nc = tc.nc
     weights = (W0, W1, W2, W3)
-    steps = [(l, third) for l in SEGMENT_ORDER for third in range(THIRDS)]
+    order = [(l, third) for l in SEGMENT_ORDER for third in range(THIRDS)]
+    slots = 2 * len(order)
 
     with ExitStack() as ctx:
         keep = ctx.enter_context(tc.tile_pool(name="keep", bufs=1))
@@ -65,6 +66,11 @@ def tile_so3_linear_pa_kernel(tc, x, W0, W1, W2, W3, bias, out):
         w_sorted = {}
         w_grouped = {}
         w_packed = {}
+        results = {}
+        sums = {}
+
+        def share(calls, k, n):
+            return calls[k * len(calls) // n : (k + 1) * len(calls) // n]
 
         def turn(words_of, columns, grouped, drain):
             bank = banks.tile([P, 2, HALVES, P], F32, tag="bank")
@@ -74,7 +80,7 @@ def tile_so3_linear_pa_kernel(tc, x, W0, W1, W2, W3, bias, out):
             drain(out=grouped, in_=bank[:, :columns].rearrange("p s u r -> p s r u"))
 
         def load_x(q):
-            l, g = steps[q]
+            l, g = order[q]
             d = IRREP_DIMS[l]
             first = SEGMENT_START[l] + g * K_PASS * d
             raw = stream.tile([P, K_PASS * d], BF16, name="x_raw", bufs=3)
@@ -82,7 +88,7 @@ def tile_so3_linear_pa_kernel(tc, x, W0, W1, W2, W3, bias, out):
             x_raw[q] = raw
 
         def split_x(q):
-            d = IRREP_DIMS[steps[q][0]]
+            d = IRREP_DIMS[order[q][0]]
             split = stream.tile([P, d, K_PASS], BF16, name="x_split", bufs=2)
             by_component = x_raw[q][:].rearrange("p (c u v i) -> p c u v i", c=BLOCKS, u=HALVES, i=d)
             parts = -(-d // 4)
@@ -94,12 +100,14 @@ def tile_so3_linear_pa_kernel(tc, x, W0, W1, W2, W3, bias, out):
                 )
             x_split[q] = split
 
-        def turn_x(q):
-            d = IRREP_DIMS[steps[q][0]]
+        def turn_x(q, part):
+            d = IRREP_DIMS[order[q][0]]
+            if part == 0:
+                grouped = stream.tile([P, d * K_PASS], BF16, name="x_grouped", align_bytes=64)
+                x_grouped[q] = grouped
             words = x_split[q][:].rearrange("p i m -> p (i m)").bitcast(F32)
-            grouped = stream.tile([P, d * K_PASS], BF16, name="x_grouped", align_bytes=64)
-            grouped_words = grouped[:].bitcast(F32)
-            for i in range(0, d, 2):
+            grouped_words = x_grouped[q][:].bitcast(F32)
+            for i in share(list(range(0, d, 2)), part, 2):
                 n = min(2, d - i)
                 turn(
                     lambda s, u: words[:, (i + s) * PASS_WORDS + u * P : (i + s) * PASS_WORDS + (u + 1) * P],
@@ -107,87 +115,87 @@ def tile_so3_linear_pa_kernel(tc, x, W0, W1, W2, W3, bias, out):
                     grouped_words[:, i * PASS_WORDS : (i + n) * PASS_WORDS].rearrange(
                         "p (s r u) -> p s r u", s=n, u=HALVES
                     ),
-                    nc.vector.tensor_copy,
+                    nc.scalar.copy,
                 )
-            x_grouped[q] = grouped
 
         def quantize_x(q):
-            l, g = steps[q]
+            l, g = order[q]
             d = IRREP_DIMS[l]
-            for i in range(0, d, 4):
-                n = min(4, d - i)
-                for a, b in ((i, i + n),) if n != 3 else ((i, i + 2), (i + 2, i + 3)):
-                    nc.vector.quantize_mx(
-                        out=x_codes[l][:, g, a * P : b * P].bitcast(FP8X4),
-                        scales=x_scales[l][:, g, a * P : b * P],
-                        in_=x_grouped[q][:, a * K_PASS : b * K_PASS],
-                    )
+            a = 0
+            while a < d:
+                b = a + (4 if d - a >= 4 else 2 if d - a >= 2 else 1)
+                nc.vector.quantize_mx(
+                    out=x_codes[l][:, g, a * P : b * P].bitcast(FP8X4),
+                    scales=x_scales[l][:, g, a * P : b * P],
+                    in_=x_grouped[q][:, a * K_PASS : b * K_PASS],
+                )
+                a = b
 
-        def load_w(q):
-            l, c = steps[q]
-            raw = stream.tile([P, ROWS * CHANNELS], BF16, name="w_raw", bufs=3)
-            nc.sync.dma_start(
-                out=raw[:],
-                in_=weights[l][c * CHUNK : (c + 1) * CHUNK, :].rearrange("(j r) m -> j (r m)", r=ROWS),
-            )
-            w_raw[q] = raw
+        def load_w(h):
+            l, c = order[h // 2]
+            raw = stream.tile([P, 2 * CHANNELS], BF16, name="w_raw", bufs=6)
+            rows = weights[l][c * CHUNK : (c + 1) * CHUNK, :].rearrange("(j h r) m -> h j (r m)", h=2, r=2)
+            nc.sync.dma_start(out=raw[:], in_=rows[h % 2])
+            w_raw[h] = raw
 
-        def sort_w(q):
-            result = stream.tile([P, ROWS * THIRDS, HALVES, P], F32, name="w_sorted")
+        def sort_w(h):
+            result = stream.tile([P, 2 * THIRDS, HALVES, P], F32, name="w_sorted", bufs=3)
             nc.vector.tensor_copy(
-                out=result[:].rearrange("p t u (c v) -> p (t u) c v", v=RUN // 2),
-                in_=w_raw[q][:].bitcast(F32).rearrange("p (t c u v) -> p t u c v", t=ROWS * THIRDS, u=HALVES, v=RUN // 2),
+                out=result[:].rearrange("p t u (c v) -> p t u c v", v=RUN // 2),
+                in_=w_raw[h][:].bitcast(F32).rearrange("p (t c u v) -> p t u c v", t=2 * THIRDS, u=HALVES, v=RUN // 2),
             )
-            w_sorted[q] = result
+            w_sorted[h] = result
 
-        def turn_w(q):
-            words = w_sorted[q]
-            grouped = stream.tile([P, THIRDS * CHUNK * 4], BF16, name="w_grouped", align_bytes=64)
-            grouped_words = grouped[:].bitcast(F32)
+        def turn_w(h):
+            words = w_sorted[h]
+            grouped = stream.tile([P, THIRDS, 2 * P * 4], BF16, name="w_grouped", bufs=3, align_bytes=64)
             for g in range(THIRDS):
-                for r in range(0, ROWS, 2):
-                    first = (g * CHUNK + r * P) * HALVES
-                    turn(
-                        lambda s, u: words[:, (r + s) * THIRDS + g, u, :],
-                        2,
-                        grouped_words[:, first : first + 2 * P * HALVES].rearrange(
-                            "p (s r u) -> p s r u", s=2, u=HALVES
-                        ),
-                        nc.scalar.copy,
-                    )
-            w_grouped[q] = grouped
+                turn(
+                    lambda s, u: words[:, s * THIRDS + g, u, :],
+                    2,
+                    grouped[:, g, :].bitcast(F32).rearrange("p (s r u) -> p s r u", s=2, u=HALVES),
+                    nc.scalar.copy,
+                )
+            w_grouped[h] = grouped
 
-        def quantize_w(q):
-            codes = stream.tile([P, THIRDS, CHUNK], U32, name="w_codes", bufs=3, align_bytes=64)
-            scales = stream.tile([P, THIRDS, CHUNK], U8, name="w_scales", bufs=3, align_bytes=64)
+        def quantize_w(h):
+            codes = stream.tile([P, THIRDS, 2 * P], U32, name="w_codes", bufs=4, align_bytes=64)
+            scales = stream.tile([P, THIRDS, 2 * P], U8, name="w_scales", bufs=4, align_bytes=64)
             for g in range(THIRDS):
                 nc.vector.quantize_mx(
-                    out=codes[:, g, :].bitcast(FP8X4),
-                    scales=scales[:, g, :],
-                    in_=w_grouped[q][:, g * CHUNK * 4 : (g + 1) * CHUNK * 4],
+                    out=codes[:, g, :].bitcast(FP8X4), scales=scales[:, g, :], in_=w_grouped[h][:, g, :]
                 )
-            w_packed[q] = (codes, scales)
+            w_packed[h] = (codes, scales)
 
-        def multiply(q):
-            l, c = steps[q]
+        def multiply(h):
+            q = h // 2
+            l, c = order[q]
             d = IRREP_DIMS[l]
-            codes, scales = w_packed[q]
-            result = stream.tile([P, CHUNK * d], F32, name="result")
-            lines = result[:].rearrange("p (j k s) -> p j k s", k=d, s=LINE)
-            for k in range(d):
-                acc = banks.tile([P, LINE, P], F32, tag="bank")
-                for s in range(LINE):
-                    r, i = divmod(LINE * k + s, d)
-                    for g in range(THIRDS):
-                        nc.tensor.matmul_mx(
-                            out=acc[:, s, :],
-                            lhsT=x_codes[l][:, g, i * P : (i + 1) * P].bitcast(FP8X4),
-                            lhsT_scale=x_scales[l][:, g, i * P : (i + 1) * P],
-                            rhs=codes[:, g, r * P : (r + 1) * P].bitcast(FP8X4),
-                            rhs_scale=scales[:, g, r * P : (r + 1) * P],
-                            start=(g == 0),
-                            stop=(g == THIRDS - 1),
-                        )
+            codes, scales = w_packed[h]
+            if h % 2 == 0:
+                result = stream.tile([P, CHUNK * d], F32, name="result")
+                results[q] = result
+            lines = results[q][:].rearrange("p (j k s) -> p j k s", k=d, s=LINE)
+            for f in range(h % 2 * 2 * d, (h % 2 + 1) * 2 * d):
+                k, s = divmod(f, LINE)
+                r, i = divmod(f, d)
+                column = (r - h % 2 * 2) * P
+                if s == 0:
+                    acc = banks.tile([P, LINE, P], F32, tag="bank")
+                    sums[q] = acc
+                acc = sums[q]
+                for g in range(THIRDS):
+                    nc.tensor.matmul_mx(
+                        out=acc[:, s, :],
+                        lhsT=x_codes[l][:, g, i * P : (i + 1) * P].bitcast(FP8X4),
+                        lhsT_scale=x_scales[l][:, g, i * P : (i + 1) * P],
+                        rhs=codes[:, g, column : column + P].bitcast(FP8X4),
+                        rhs_scale=scales[:, g, column : column + P],
+                        start=(g == 0),
+                        stop=(g == THIRDS - 1),
+                    )
+                if s < LINE - 1:
+                    continue
                 by_line = acc[:].rearrange("p s j -> p j s")
                 if l == 0:
                     nc.vector.tensor_tensor(
@@ -196,26 +204,37 @@ def tile_so3_linear_pa_kernel(tc, x, W0, W1, W2, W3, bias, out):
                         in1=bias_rows[:, c * CHUNK : (c + 1) * CHUNK].rearrange("p (j s) -> p j s", s=LINE),
                         op=mybir.AluOpType.add,
                     )
+                elif k % 2:
+                    nc.vector.tensor_copy(out=lines[:, :, k, :], in_=by_line)
                 else:
                     nc.scalar.copy(out=lines[:, :, k, :], in_=by_line)
-            first = SEGMENT_START[l] + c * CHUNK * d
-            nc.scalar.dma_start(out=out[:, first : first + CHUNK * d], in_=result[:])
+            if h % 2:
+                first = SEGMENT_START[l] + c * CHUNK * d
+                nc.scalar.dma_start(out=out[:, first : first + CHUNK * d], in_=results[q][:])
 
-        last = len(steps)
+        def piece_at(h, lead):
+            q, odd = divmod(h + lead, 2)
+            return [q] if not odd and 0 <= q < len(order) else []
 
-        def at(stage, q):
-            if 0 <= q < last:
-                stage(q)
-
-        for now in range(-X_LOAD_LEAD, last):
-            at(load_w, now + W_LOAD_LEAD)
-            at(load_x, now + X_LOAD_LEAD)
-            if now + X_LOAD_LEAD == last:
+        for h in range(-max(X_LOAD, W_LOAD), slots):
+            for q in piece_at(h, X_LOAD):
+                load_x(q)
+            if 0 <= h + W_LOAD < slots:
+                load_w(h + W_LOAD)
+            if h + X_LOAD == slots:
                 nc.sync.dma_start(out=bias_rows[:], in_=bias.partition_broadcast(P))
-            at(sort_w, now + W_SORT_LEAD)
-            at(turn_w, now + W_TURN_LEAD)
-            at(turn_x, now + X_TURN_LEAD)
-            at(quantize_w, now + W_QUANT_LEAD)
-            at(quantize_x, now + X_QUANT_LEAD)
-            at(split_x, now + X_SPLIT_LEAD)
-            at(multiply, now)
+            if 0 <= h + W_TURN < slots:
+                turn_w(h + W_TURN)
+            for part in (0, 1):
+                for q in piece_at(h - part, X_TURN):
+                    turn_x(q, part)
+            if 0 <= h + W_QUANT < slots:
+                quantize_w(h + W_QUANT)
+            for q in piece_at(h, X_QUANT):
+                quantize_x(q)
+            if 0 <= h + W_SORT < slots:
+                sort_w(h + W_SORT)
+            for q in piece_at(h, X_SPLIT):
+                split_x(q)
+            if 0 <= h:
+                multiply(h)

@@ -26,9 +26,9 @@ LINE = 4
 SEGMENT_ORDER = (1, 2, 3, 0)
 
 W_LOAD = 6
-W_SORT = 3
-W_TURN = 2
-W_QUANT = 1
+W_SORT = 4
+W_TURN = 3
+W_QUANT = 2
 X_LOAD = 10
 X_SPLIT = 8
 X_TURN = 7
@@ -159,8 +159,8 @@ def tile_so3_linear_pa_kernel(tc, x, W0, W1, W2, W3, bias, out):
             w_grouped[h] = grouped
 
         def quantize_w(h):
-            codes = stream.tile([P, THIRDS, 2 * P], U32, name="w_codes", bufs=4, align_bytes=64)
-            scales = stream.tile([P, THIRDS, 2 * P], U8, name="w_scales", bufs=4, align_bytes=64)
+            codes = stream.tile([P, THIRDS, 2 * P], U32, name="w_codes", bufs=8, align_bytes=64)
+            scales = stream.tile([P, THIRDS, 2 * P], U8, name="w_scales", bufs=8, align_bytes=64)
             for g in range(THIRDS):
                 nc.vector.quantize_mx(
                     out=codes[:, g, :].bitcast(FP8X4), scales=scales[:, g, :], in_=w_grouped[h][:, g, :]
@@ -173,7 +173,7 @@ def tile_so3_linear_pa_kernel(tc, x, W0, W1, W2, W3, bias, out):
             d = IRREP_DIMS[l]
             codes, scales = w_packed[h]
             if h % 2 == 0:
-                result = stream.tile([P, CHUNK * d], F32, name="result")
+                result = stream.tile([P, CHUNK * d], F32, name="result%d" % min(l, 1))
                 results[q] = result
             lines = results[q][:].rearrange("p (j k s) -> p j k s", k=d, s=LINE)
             for f in range(h % 2 * 2 * d, (h % 2 + 1) * 2 * d):
@@ -216,25 +216,28 @@ def tile_so3_linear_pa_kernel(tc, x, W0, W1, W2, W3, bias, out):
             q, odd = divmod(h + lead, 2)
             return [q] if not odd and 0 <= q < len(order) else []
 
+        def halves_at(h):
+            return [h + W_TURN] if 0 <= h + W_TURN < slots else []
+
         for h in range(-max(X_LOAD, W_LOAD), slots):
             for q in piece_at(h, X_LOAD):
                 load_x(q)
-            if 0 <= h + W_LOAD < slots:
-                load_w(h + W_LOAD)
+            for t in halves_at(h + W_LOAD - W_TURN):
+                load_w(t)
             if h + X_LOAD == slots:
                 nc.sync.dma_start(out=bias_rows[:], in_=bias.partition_broadcast(P))
-            if 0 <= h + W_TURN < slots:
-                turn_w(h + W_TURN)
+            for q in piece_at(h, X_SPLIT):
+                split_x(q)
+            for t in halves_at(h + W_SORT - W_TURN):
+                sort_w(t)
+            for q in piece_at(h, X_QUANT):
+                quantize_x(q)
+            for t in halves_at(h - W_TURN + W_QUANT):
+                quantize_w(t)
+            for t in halves_at(h):
+                turn_w(t)
             for part in (0, 1):
                 for q in piece_at(h - part, X_TURN):
                     turn_x(q, part)
-            if 0 <= h + W_QUANT < slots:
-                quantize_w(h + W_QUANT)
-            for q in piece_at(h, X_QUANT):
-                quantize_x(q)
-            if 0 <= h + W_SORT < slots:
-                sort_w(h + W_SORT)
-            for q in piece_at(h, X_SPLIT):
-                split_x(q)
             if 0 <= h:
                 multiply(h)

@@ -20,28 +20,67 @@ RUN = 16
 BLOCKS = K_PASS // (HALVES * RUN)
 PASS_WORDS = K_PASS // 2
 CHUNK = 512
-ROWS = CHUNK // P
 LINE = 4
 
-SEGMENT_ORDER = (1, 2, 3, 0)
+PHASES = (
+    ((1, 0), (1, 1), (1, 2)),
+    ((2, 0), (2, 1), (2, 2)),
+    ((3, 0), (3, 1), (3, 2)),
+    ((0, 0), (0, 1), (0, 2)),
+)
 
-W_LOAD = 6
-W_SORT = 4
-W_TURN = 3
-W_QUANT = 2
-X_LOAD = 10
-X_SPLIT = 8
-X_TURN = 7
-X_QUANT = 5
+AHEAD = 3
+END_AHEAD = 4
+LOAD = 6
+PREP = 2
+QUANT = 1
 
 FLOPS = 2 * P * sum(IRREP_DIMS) * CHANNELS * CHANNELS
+
+
+def spread(few, many):
+    result = list(many)
+    for n in reversed(range(len(few))):
+        result.insert((n + 1) * len(many) // (len(few) + 1), few[n])
+    return result
+
+
+def share(calls, k, n):
+    return calls[k * len(calls) // n : (k + 1) * len(calls) // n]
 
 
 def tile_so3_linear_pa_kernel(tc, x, W0, W1, W2, W3, bias, out):
     nc = tc.nc
     weights = (W0, W1, W2, W3)
-    order = [(l, third) for l in SEGMENT_ORDER for third in range(THIRDS)]
-    slots = 2 * len(order)
+    chunks = [chunk for phase in PHASES for chunk in phase]
+    pieces = {l: [("x", l, g) for g in range(THIRDS)] for l in (1, 2, 3)}
+    pieces[0] = [("x", 0, 0)]
+
+    def cells(h):
+        l = chunks[h // 2][0]
+        if l == 0:
+            return [(h, 0)]
+        d = IRREP_DIMS[l]
+        return [(h, f) for f in range(h % 2 * 2 * d, (h % 2 + 1) * 2 * d)]
+
+    halves = 2 * len(chunks)
+    items = pieces[1] + [("w", h) for h in range(AHEAD)]
+    shares = {}
+    first = 0
+    w_first = AHEAD
+    for p, phase in enumerate(PHASES):
+        last = first + 2 * len(phase)
+        w_end = min(halves, last + (END_AHEAD if p >= 2 else AHEAD))
+        w_items = [("w", h) for h in range(w_first, w_end)]
+        w_first = w_end
+        x_items = pieces[(2, 3, 0)[p]] if p < 3 else []
+        start = len(items)
+        items = items + spread(x_items, w_items)
+        todo = [cell for h in range(first, last) for cell in cells(h)]
+        rounds = max(len(phase) * 2, len(items) - start) if p == 3 else len(items) - start
+        for k in range(rounds):
+            shares[start + k] = share(todo, k, rounds)
+        first = last
 
     with ExitStack() as ctx:
         keep = ctx.enter_context(tc.tile_pool(name="keep", bufs=1))
@@ -55,189 +94,213 @@ def tile_so3_linear_pa_kernel(tc, x, W0, W1, W2, W3, bias, out):
         x_codes = {}
         x_scales = {}
         for l, d in enumerate(IRREP_DIMS):
-            codes = keep.tile([P, THIRDS, d * P], U32, name="x_codes%d" % l, align_bytes=64)
-            scales = keep.tile([P, THIRDS, d * P], U8, name="x_scales%d" % l, align_bytes=64)
+            codes = keep.tile([P, THIRDS * d * P], U32, name="x_codes%d" % l, align_bytes=64)
+            scales = keep.tile([P, THIRDS * d * P], U8, name="x_scales%d" % l, align_bytes=64)
             x_codes[l] = codes
             x_scales[l] = scales
-        x_raw = {}
-        x_split = {}
-        x_grouped = {}
-        w_raw = {}
-        w_sorted = {}
-        w_grouped = {}
-        w_packed = {}
+        raw_of = {}
+        sorted_of = {}
+        grouped_of = {}
+        packed_of = {}
         results = {}
         sums = {}
+        late = []
+        done = []
 
-        def share(calls, k, n):
-            return calls[k * len(calls) // n : (k + 1) * len(calls) // n]
+        def sets(item):
+            return IRREP_DIMS[item[1]] if item[1] else THIRDS
 
-        def turn(words_of, columns, grouped, drain):
+        def turn(words_of, columns, grouped):
             bank = banks.tile([P, 2, HALVES, P], F32, tag="bank")
             for s in range(columns):
                 for u in range(HALVES):
                     nc.tensor.transpose(bank[:, s, u, :], words_of(s, u), identity[:])
-            drain(out=grouped, in_=bank[:, :columns].rearrange("p s u r -> p s r u"))
+            nc.scalar.copy(out=grouped, in_=bank[:, :columns].rearrange("p s u r -> p s r u"))
 
-        def load_x(q):
-            l, g = order[q]
-            d = IRREP_DIMS[l]
-            first = SEGMENT_START[l] + g * K_PASS * d
-            raw = stream.tile([P, K_PASS * d], BF16, name="x_raw", bufs=3)
-            nc.sync.dma_start(out=raw[:], in_=x[:, first : first + K_PASS * d])
-            x_raw[q] = raw
+        def load_x(item):
+            l, g = item[1:]
+            width = sets(item) * K_PASS
+            first = SEGMENT_START[l] + g * width
+            raw = stream.tile([P, width], BF16, name="x_raw", bufs=2)
+            nc.sync.dma_start(out=raw[:], in_=x[:, first : first + width])
+            raw_of[item] = raw
 
-        def split_x(q):
-            d = IRREP_DIMS[order[q][0]]
-            split = stream.tile([P, d, K_PASS], BF16, name="x_split", bufs=2)
-            by_component = x_raw[q][:].rearrange("p (c u v i) -> p c u v i", c=BLOCKS, u=HALVES, i=d)
-            parts = -(-d // 4)
+        def split_x(item):
+            n = sets(item)
+            split = stream.tile([P, n, K_PASS], BF16, name="x_split", bufs=2)
+            sorted_of[item] = split
+            if item[1] == 0:
+                nc.vector.tensor_copy(
+                    out=split[:].rearrange("p g (u c v) -> p g u c v", u=HALVES, c=BLOCKS),
+                    in_=raw_of[item][:].rearrange("p (g c u v) -> p g u c v", g=THIRDS, c=BLOCKS, u=HALVES),
+                )
+                return
+            by_component = raw_of[item][:].rearrange("p (c u v i) -> p c u v i", c=BLOCKS, u=HALVES, i=n)
+            parts = -(-n // 4)
             for k in range(parts):
-                i0, i1 = k * d // parts, (k + 1) * d // parts
+                i0, i1 = k * n // parts, (k + 1) * n // parts
                 nc.vector.tensor_copy(
                     out=split[:, i0:i1, :].rearrange("p i (u c v) -> p c u v i", u=HALVES, c=BLOCKS),
                     in_=by_component[:, :, :, :, i0:i1],
                 )
-            x_split[q] = split
 
-        def turn_x(q, part):
-            d = IRREP_DIMS[order[q][0]]
-            if part == 0:
-                grouped = stream.tile([P, d * K_PASS], BF16, name="x_grouped", align_bytes=64)
-                x_grouped[q] = grouped
-            words = x_split[q][:].rearrange("p i m -> p (i m)").bitcast(F32)
-            grouped_words = x_grouped[q][:].bitcast(F32)
-            for i in share(list(range(0, d, 2)), part, 2):
-                n = min(2, d - i)
+        def turn_x(item):
+            n = sets(item)
+            grouped = stream.tile([P, n * K_PASS], BF16, name="x_grouped", bufs=2, align_bytes=64)
+            grouped_of[item] = grouped
+            words = sorted_of[item][:].rearrange("p i m -> p (i m)").bitcast(F32)
+            grouped_words = grouped[:].bitcast(F32)
+            for i in range(0, n, 2):
+                w = min(2, n - i)
                 turn(
                     lambda s, u: words[:, (i + s) * PASS_WORDS + u * P : (i + s) * PASS_WORDS + (u + 1) * P],
-                    n,
-                    grouped_words[:, i * PASS_WORDS : (i + n) * PASS_WORDS].rearrange(
-                        "p (s r u) -> p s r u", s=n, u=HALVES
+                    w,
+                    grouped_words[:, i * PASS_WORDS : (i + w) * PASS_WORDS].rearrange(
+                        "p (s r u) -> p s r u", s=w, u=HALVES
                     ),
-                    nc.scalar.copy,
                 )
 
-        def quantize_x(q):
-            l, g = order[q]
-            d = IRREP_DIMS[l]
+        def quantize_x(item):
+            l, g = item[1:]
+            n = sets(item)
             a = 0
-            while a < d:
-                b = a + (4 if d - a >= 4 else 2 if d - a >= 2 else 1)
+            while a < n:
+                b = a + (4 if n - a >= 4 else 2 if n - a >= 2 else 1)
+                first = (g * n + a) * P
+                last = (g * n + b) * P
                 nc.vector.quantize_mx(
-                    out=x_codes[l][:, g, a * P : b * P].bitcast(FP8X4),
-                    scales=x_scales[l][:, g, a * P : b * P],
-                    in_=x_grouped[q][:, a * K_PASS : b * K_PASS],
+                    out=x_codes[l][:, first:last].bitcast(FP8X4),
+                    scales=x_scales[l][:, first:last],
+                    in_=grouped_of[item][:, a * K_PASS : b * K_PASS],
                 )
                 a = b
 
-        def load_w(h):
-            l, c = order[h // 2]
-            raw = stream.tile([P, 2 * CHANNELS], BF16, name="w_raw", bufs=6)
-            rows = weights[l][c * CHUNK : (c + 1) * CHUNK, :].rearrange("(j h r) m -> h j (r m)", h=2, r=2)
+        def load_w(item):
+            h = item[1]
+            l, c = chunks[h // 2]
+            raw = stream.tile([P, 2, CHANNELS], BF16, name="w_raw", bufs=6)
+            rows = weights[l][c * CHUNK : (c + 1) * CHUNK, :].rearrange(
+                "(h r j) m -> h j r m" if l == 0 else "(j h r) m -> h j r m", h=2, r=2
+            )
             nc.sync.dma_start(out=raw[:], in_=rows[h % 2])
-            w_raw[h] = raw
+            raw_of[item] = raw
 
-        def sort_w(h):
+        def sort_w(item):
             result = stream.tile([P, 2 * THIRDS, HALVES, P], F32, name="w_sorted", bufs=3)
+            raw = raw_of[item][:].rearrange("p r m -> p (r m)").bitcast(F32)
             nc.vector.tensor_copy(
                 out=result[:].rearrange("p t u (c v) -> p t u c v", v=RUN // 2),
-                in_=w_raw[h][:].bitcast(F32).rearrange("p (t c u v) -> p t u c v", t=2 * THIRDS, u=HALVES, v=RUN // 2),
+                in_=raw.rearrange("p (t c u v) -> p t u c v", t=2 * THIRDS, u=HALVES, v=RUN // 2),
             )
-            w_sorted[h] = result
+            sorted_of[item] = result
 
-        def turn_w(h):
-            words = w_sorted[h]
+        def turn_w(item):
+            words = sorted_of[item]
             grouped = stream.tile([P, THIRDS, 2 * P * 4], BF16, name="w_grouped", bufs=3, align_bytes=64)
             for g in range(THIRDS):
                 turn(
                     lambda s, u: words[:, s * THIRDS + g, u, :],
                     2,
                     grouped[:, g, :].bitcast(F32).rearrange("p (s r u) -> p s r u", s=2, u=HALVES),
-                    nc.scalar.copy,
                 )
-            w_grouped[h] = grouped
+            grouped_of[item] = grouped
 
-        def quantize_w(h):
-            codes = stream.tile([P, THIRDS, 2 * P], U32, name="w_codes", bufs=8, align_bytes=64)
-            scales = stream.tile([P, THIRDS, 2 * P], U8, name="w_scales", bufs=8, align_bytes=64)
+        def quantize_w(item):
+            codes = stream.tile([P, THIRDS, 2 * P], U32, name="w_codes", bufs=10, align_bytes=64)
+            scales = stream.tile([P, THIRDS, 2 * P], U8, name="w_scales", bufs=10, align_bytes=64)
             for g in range(THIRDS):
                 nc.vector.quantize_mx(
-                    out=codes[:, g, :].bitcast(FP8X4), scales=scales[:, g, :], in_=w_grouped[h][:, g, :]
+                    out=codes[:, g, :].bitcast(FP8X4), scales=scales[:, g, :], in_=grouped_of[item][:, g, :]
                 )
-            w_packed[h] = (codes, scales)
+            packed_of[item[1]] = (codes, scales)
 
-        def multiply(h):
+        def load(item):
+            (load_x if item[0] == "x" else load_w)(item)
+
+        def prepare(item):
+            (split_x if item[0] == "x" else sort_w)(item)
+
+        def turn_item(item):
+            (turn_x if item[0] == "x" else turn_w)(item)
+
+        def quantize(item):
+            (quantize_x if item[0] == "x" else quantize_w)(item)
+
+        def mx_pass(acc, l, g, i, h, column, width):
+            codes, scales = packed_of[h]
+            a = (g * IRREP_DIMS[l] + i) * P
+            nc.tensor.matmul_mx(
+                out=acc,
+                lhsT=x_codes[l][:, a : a + P].bitcast(FP8X4),
+                lhsT_scale=x_scales[l][:, a : a + P],
+                rhs=codes[:, g, column : column + width].bitcast(FP8X4),
+                rhs_scale=scales[:, g, column : column + width],
+                start=(g == 0),
+                stop=(g == THIRDS - 1),
+            )
+
+        def multiply(h, f):
             q = h // 2
-            l, c = order[q]
+            l, c = chunks[q]
             d = IRREP_DIMS[l]
-            codes, scales = w_packed[h]
-            if h % 2 == 0:
-                result = stream.tile([P, CHUNK * d], F32, name="result%d" % min(l, 1))
-                results[q] = result
-            lines = results[q][:].rearrange("p (j k s) -> p j k s", k=d, s=LINE)
-            for f in range(h % 2 * 2 * d, (h % 2 + 1) * 2 * d):
-                k, s = divmod(f, LINE)
-                r, i = divmod(f, d)
-                column = (r - h % 2 * 2) * P
-                if s == 0:
-                    acc = banks.tile([P, LINE, P], F32, tag="bank")
-                    sums[q] = acc
-                acc = sums[q]
+            if l == 0:
+                acc = banks.tile([P, 2 * P], F32, tag="bank")
                 for g in range(THIRDS):
-                    nc.tensor.matmul_mx(
-                        out=acc[:, s, :],
-                        lhsT=x_codes[l][:, g, i * P : (i + 1) * P].bitcast(FP8X4),
-                        lhsT_scale=x_scales[l][:, g, i * P : (i + 1) * P],
-                        rhs=codes[:, g, column : column + P].bitcast(FP8X4),
-                        rhs_scale=scales[:, g, column : column + P],
-                        start=(g == 0),
-                        stop=(g == THIRDS - 1),
-                    )
-                if s < LINE - 1:
-                    continue
+                    mx_pass(acc[:], 0, g, 0, h, 0, 2 * P)
+                result = stream.tile([P, 2 * P], F32, name="result0", bufs=6)
+                first = c * CHUNK + h % 2 * 2 * P
+                late.append((result[:], acc[:], bias_rows[:, first : first + 2 * P]))
+                results[h] = (first, result)
+                done.append(h)
+                return
+            k, s = divmod(f, LINE)
+            r, i = divmod(f, d)
+            if f == 0:
+                result = stream.tile([P, CHUNK * d], F32, name="result")
+                results[h + 1] = (SEGMENT_START[l] + c * CHUNK * d, result)
+            if s == 0:
+                acc = banks.tile([P, LINE, P], F32, tag="bank")
+                sums[q] = acc
+            acc = sums[q]
+            for g in range(THIRDS):
+                mx_pass(acc[:, s, :], l, g, i, h, r % 2 * P, P)
+            if s == LINE - 1:
+                lines = results[2 * q + 1][1][:].rearrange("p (j k s) -> p j k s", k=d, s=LINE)
                 by_line = acc[:].rearrange("p s j -> p j s")
-                if l == 0:
-                    nc.vector.tensor_tensor(
-                        out=lines[:, :, k, :],
-                        in0=by_line,
-                        in1=bias_rows[:, c * CHUNK : (c + 1) * CHUNK].rearrange("p (j s) -> p j s", s=LINE),
-                        op=mybir.AluOpType.add,
-                    )
-                elif k % 2:
-                    nc.vector.tensor_copy(out=lines[:, :, k, :], in_=by_line)
+                if k % 2:
+                    late.append((lines[:, :, k, :], by_line, None))
                 else:
                     nc.scalar.copy(out=lines[:, :, k, :], in_=by_line)
-            if h % 2:
-                first = SEGMENT_START[l] + c * CHUNK * d
-                nc.scalar.dma_start(out=out[:, first : first + CHUNK * d], in_=results[q][:])
+            if f == 4 * d - 1:
+                done.append(h)
 
-        def piece_at(h, lead):
-            q, odd = divmod(h + lead, 2)
-            return [q] if not odd and 0 <= q < len(order) else []
+        def drain_late():
+            for target, source, addend in late:
+                if addend is None:
+                    nc.vector.tensor_copy(out=target, in_=source)
+                else:
+                    nc.vector.tensor_tensor(out=target, in0=source, in1=addend, op=mybir.AluOpType.add)
+            late.clear()
 
-        def halves_at(h):
-            return [h + W_TURN] if 0 <= h + W_TURN < slots else []
+        def store(h):
+            first, result = results[h]
+            width = result.shape[1]
+            nc.scalar.dma_start(out=out[:, first : first + width], in_=result[:])
 
-        for h in range(-max(X_LOAD, W_LOAD), slots):
-            for q in piece_at(h, X_LOAD):
-                load_x(q)
-            for t in halves_at(h + W_LOAD - W_TURN):
-                load_w(t)
-            if h + X_LOAD == slots:
+        for j in range(-LOAD, max(shares) + 1):
+            if 0 <= j + LOAD < len(items):
+                load(items[j + LOAD])
+            if j + LOAD == len(items):
                 nc.sync.dma_start(out=bias_rows[:], in_=bias.partition_broadcast(P))
-            for q in piece_at(h, X_SPLIT):
-                split_x(q)
-            for t in halves_at(h + W_SORT - W_TURN):
-                sort_w(t)
-            for q in piece_at(h, X_QUANT):
-                quantize_x(q)
-            for t in halves_at(h - W_TURN + W_QUANT):
-                quantize_w(t)
-            for t in halves_at(h):
-                turn_w(t)
-            for part in (0, 1):
-                for q in piece_at(h - part, X_TURN):
-                    turn_x(q, part)
-            if 0 <= h:
-                multiply(h)
+            if 0 <= j - QUANT < len(items):
+                quantize(items[j - QUANT])
+            if 0 <= j + PREP < len(items):
+                prepare(items[j + PREP])
+            if 0 <= j < len(items):
+                turn_item(items[j])
+            for cell in shares.get(j, []):
+                multiply(*cell)
+            drain_late()
+            for h in done:
+                store(h)
+            done.clear()

@@ -29,7 +29,7 @@ PHASES = (
     ((0, 0), (0, 1), (0, 2)),
 )
 
-AHEAD = 3
+AHEAD = 2
 END_AHEAD = 4
 LOAD = 6
 PREP = 2
@@ -121,7 +121,7 @@ def tile_so3_linear_pa_kernel(tc, x, W0, W1, W2, W3, bias, out):
             l, g = item[1:]
             width = sets(item) * K_PASS
             first = SEGMENT_START[l] + g * width
-            raw = stream.tile([P, width], BF16, name="x_raw", bufs=2)
+            raw = stream.tile([P, width], BF16, name="x_raw", bufs=3)
             nc.sync.dma_start(out=raw[:], in_=x[:, first : first + width])
             raw_of[item] = raw
 

@@ -178,7 +178,7 @@ def tile_so3_linear_pa_kernel(tc, x, W0, W1, W2, W3, bias, out):
         def load_w(item):
             h = item[1]
             l, c = chunks[h // 2]
-            raw = stream.tile([P, 2, CHANNELS], BF16, name="w_raw", bufs=6)
+            raw = stream.tile([P, 2, CHANNELS], BF16, name="w_raw", bufs=5)
             rows = weights[l][c * CHUNK : (c + 1) * CHUNK, :].rearrange(
                 "(h r j) m -> h j r m" if l == 0 else "(j h r) m -> h j r m", h=2, r=2
             )
@@ -206,8 +206,8 @@ def tile_so3_linear_pa_kernel(tc, x, W0, W1, W2, W3, bias, out):
             grouped_of[item] = grouped
 
         def quantize_w(item):
-            codes = stream.tile([P, THIRDS, 2 * P], U32, name="w_codes", bufs=10, align_bytes=64)
-            scales = stream.tile([P, THIRDS, 2 * P], U8, name="w_scales", bufs=10, align_bytes=64)
+            codes = stream.tile([P, THIRDS, 2 * P], U32, name="w_codes", bufs=7, align_bytes=64)
+            scales = stream.tile([P, THIRDS, 2 * P], U8, name="w_scales", bufs=7, align_bytes=64)
             for g in range(THIRDS):
                 nc.vector.quantize_mx(
                     out=codes[:, g, :].bitcast(FP8X4), scales=scales[:, g, :], in_=grouped_of[item][:, g, :]
@@ -256,7 +256,7 @@ def tile_so3_linear_pa_kernel(tc, x, W0, W1, W2, W3, bias, out):
             k, s = divmod(f, LINE)
             r, i = divmod(f, d)
             if f == 0:
-                result = stream.tile([P, CHUNK * d], F32, name="result")
+                result = stream.tile([P, CHUNK * d], F32, name="result1" if l == 1 else "result", bufs=3 if l == 1 else 2)
                 results[h + 1] = (SEGMENT_START[l] + c * CHUNK * d, result)
             if s == 0:
                 acc = banks.tile([P, LINE, P], F32, tag="bank")

from contextlib import ExitStack

import concourse.mybir as mybir
from concourse.masks import make_identity

F32 = mybir.dt.float32
BF16 = mybir.dt.bfloat16
U32 = mybir.dt.uint32
U8 = mybir.dt.uint8
FP8X4 = mybir.dt.float8_e4m3fn_x4

P = 128
CHANNELS = 1536
IRREP_DIMS = (1, 3, 5, 7)
SEGMENT_START = (0, 1536, 6144, 13824)
K_PASS = 512
THIRDS = CHANNELS // K_PASS
HALVES = 2
RUN = 16
BLOCKS = K_PASS // (HALVES * RUN)
PASS_WORDS = K_PASS // 2
CHUNK = 512
LINE = 4

PHASES = (
    ((1, 0), (1, 1), (1, 2)),
    ((2, 0), (2, 1), (2, 2)),
    ((3, 0), (3, 1), (3, 2)),
    ((0, 0), (0, 1), (0, 2)),
)

AHEAD = 2
END_AHEAD = 4
LOAD = 6
PREP = 2
QUANT = 1

FLOPS = 2 * P * sum(IRREP_DIMS) * CHANNELS * CHANNELS


def spread(few, many):
    result = list(many)
    for n in reversed(range(len(few))):
        result.insert((n + 1) * len(many) // (len(few) + 1), few[n])
    return result


def share(calls, k, n):
    return calls[k * len(calls) // n : (k + 1) * len(calls) // n]


def tile_so3_linear_pa_kernel(tc, x, W0, W1, W2, W3, bias, out):
    nc = tc.nc
    weights = (W0, W1, W2, W3)
    chunks = [chunk for phase in PHASES for chunk in phase]
    pieces = {l: [("x", l, g) for g in range(THIRDS)] for l in (1, 2, 3)}
    pieces[0] = [("x", 0, 0)]

    def cells(h):
        l = chunks[h // 2][0]
        if l == 0:
            return [(h, 0)]
        d = IRREP_DIMS[l]
        return [(h, f) for f in range(h % 2 * 2 * d, (h % 2 + 1) * 2 * d)]

    halves = 2 * len(chunks)
    items = pieces[1] + [("w", h) for h in range(AHEAD)]
    shares = {}
    first = 0
    w_first = AHEAD
    for p, phase in enumerate(PHASES):
        last = first + 2 * len(phase)
        w_end = min(halves, last + (END_AHEAD if p >= 2 else AHEAD))
        w_items = [("w", h) for h in range(w_first, w_end)]
        w_first = w_end
        x_items = pieces[(2, 3, 0)[p]] if p < 3 else []
        start = len(items)
        items = items + spread(x_items, w_items)
        todo = [cell for h in range(first, last) for cell in cells(h)]
        rounds = max(len(phase) * 2, len(items) - start) if p == 3 else len(items) - start
        for k in range(rounds):
            shares[start + k] = share(todo, k, rounds)
        first = last

    with ExitStack() as ctx:
        keep = ctx.enter_context(tc.tile_pool(name="keep", bufs=1))
        stream = ctx.enter_context(tc.tile_pool(name="stream", bufs=2))
        banks = ctx.enter_context(tc.psum_pool(name="banks", bufs=8))
        ctx.enter_context(tc.manual_schedule())

        identity = keep.tile([P, P], F32)
        make_identity(nc, identity[:])
        bias_rows = keep.tile([P, CHANNELS], BF16)
        x_codes = {}
        x_scales = {}
        for l, d in enumerate(IRREP_DIMS):
            codes = keep.tile([P, THIRDS * d * P], U32, name="x_codes%d" % l, align_bytes=64)
            scales = keep.tile([P, THIRDS * d * P], U8, name="x_scales%d" % l, align_bytes=64)
            x_codes[l] = codes
            x_scales[l] = scales
        raw_of = {}
        sorted_of = {}
        grouped_of = {}
        packed_of = {}
        results = {}
        sums = {}
        late = []
        done = []

        def sets(item):
            return IRREP_DIMS[item[1]] if item[1] else THIRDS

        def turn(words_of, columns, grouped):
            bank = banks.tile([P, 2, HALVES, P], F32, tag="bank")
            for s in range(columns):
                for u in range(HALVES):
                    nc.tensor.transpose(bank[:, s, u, :], words_of(s, u), identity[:])
            nc.scalar.copy(out=grouped, in_=bank[:, :columns].rearrange("p s u r -> p s r u"))

        def load_x(item):
            l, g = item[1:]
            width = sets(item) * K_PASS
            first = SEGMENT_START[l] + g * width
            raw = stream.tile([P, width], BF16, name="x_raw", bufs=3)
            nc.sync.dma_start(out=raw[:], in_=x[:, first : first + width])
            raw_of[item] = raw

        def split_x(item):
            n = sets(item)
            split = stream.tile([P, n, K_PASS], BF16, name="x_split", bufs=2)
            sorted_of[item] = split
            if item[1] == 0:
                nc.vector.tensor_copy(
                    out=split[:].rearrange("p g (u c v) -> p g u c v", u=HALVES, c=BLOCKS),
                    in_=raw_of[item][:].rearrange("p (g c u v) -> p g u c v", g=THIRDS, c=BLOCKS, u=HALVES),
                )
                return
            by_component = raw_of[item][:].rearrange("p (c u v i) -> p c u v i", c=BLOCKS, u=HALVES, i=n)
            parts = -(-n // 4)
            for k in range(parts):
                i0, i1 = k * n // parts, (k + 1) * n // parts
                nc.vector.tensor_copy(
                    out=split[:, i0:i1, :].rearrange("p i (u c v) -> p c u v i", u=HALVES, c=BLOCKS),
                    in_=by_component[:, :, :, :, i0:i1],
                )

        def turn_x(item):
            n = sets(item)
            grouped = stream.tile([P, n * K_PASS], BF16, name="x_grouped", bufs=2, align_bytes=64)
            grouped_of[item] = grouped
            words = sorted_of[item][:].rearrange("p i m -> p (i m)").bitcast(F32)
            grouped_words = grouped[:].bitcast(F32)
            for i in range(0, n, 2):
                w = min(2, n - i)
                turn(
                    lambda s, u: words[:, (i + s) * PASS_WORDS + u * P : (i + s) * PASS_WORDS + (u + 1) * P],
                    w,
                    grouped_words[:, i * PASS_WORDS : (i + w) * PASS_WORDS].rearrange(
                        "p (s r u) -> p s r u", s=w, u=HALVES
                    ),
                )

        def quantize_x(item):
            l, g = item[1:]
            n = sets(item)
            a = 0
            while a < n:
                b = a + (4 if n - a >= 4 else 2 if n - a >= 2 else 1)
                first = (g * n + a) * P
                last = (g * n + b) * P
                nc.vector.quantize_mx(
                    out=x_codes[l][:, first:last].bitcast(FP8X4),
                    scales=x_scales[l][:, first:last],
                    in_=grouped_of[item][:, a * K_PASS : b * K_PASS],
                )
                a = b

        def load_w(item):
            h = item[1]
            l, c = chunks[h // 2]
            raw = stream.tile([P, 2, CHANNELS], BF16, name="w_raw", bufs=5)
            rows = weights[l][c * CHUNK : (c + 1) * CHUNK, :].rearrange(
                "(h r j) m -> h j r m" if l == 0 else "(j h r) m -> h j r m", h=2, r=2
            )
            nc.sync.dma_start(out=raw[:], in_=rows[h % 2])
            raw_of[item] = raw

        def sort_w(item):
            result = stream.tile([P, 2 * THIRDS, HALVES, P], F32, name="w_sorted", bufs=3)
            raw = raw_of[item][:].rearrange("p r m -> p (r m)").bitcast(F32)
            nc.vector.tensor_copy(
                out=result[:].rearrange("p t u (c v) -> p t u c v", v=RUN // 2),
                in_=raw.rearrange("p (t c u v) -> p t u c v", t=2 * THIRDS, u=HALVES, v=RUN // 2),
            )
            sorted_of[item] = result

        def turn_w(item):
            words = sorted_of[item]
            grouped = stream.tile([P, THIRDS, 2 * P * 4], BF16, name="w_grouped", bufs=3, align_bytes=64)
            for g in range(THIRDS):
                turn(
                    lambda s, u: words[:, s * THIRDS + g, u, :],
                    2,
                    grouped[:, g, :].bitcast(F32).rearrange("p (s r u) -> p s r u", s=2, u=HALVES),
                )
            grouped_of[item] = grouped

        def quantize_w(item):
            codes = stream.tile([P, THIRDS, 2 * P], U32, name="w_codes", bufs=7, align_bytes=64)
            scales = stream.tile([P, THIRDS, 2 * P], U8, name="w_scales", bufs=7, align_bytes=64)
            for g in range(THIRDS):
                nc.vector.quantize_mx(
                    out=codes[:, g, :].bitcast(FP8X4), scales=scales[:, g, :], in_=grouped_of[item][:, g, :]
                )
            packed_of[item[1]] = (codes, scales)

        def load(item):
            (load_x if item[0] == "x" else load_w)(item)

        def prepare(item):
            (split_x if item[0] == "x" else sort_w)(item)

        def turn_item(item):
            (turn_x if item[0] == "x" else turn_w)(item)

        def quantize(item):
            (quantize_x if item[0] == "x" else quantize_w)(item)

        def mx_pass(acc, l, g, i, h, column, width):
            codes, scales = packed_of[h]
            a = (g * IRREP_DIMS[l] + i) * P
            nc.tensor.matmul_mx(
                out=acc,
                lhsT=x_codes[l][:, a : a + P].bitcast(FP8X4),
                lhsT_scale=x_scales[l][:, a : a + P],
                rhs=codes[:, g, column : column + width].bitcast(FP8X4),
                rhs_scale=scales[:, g, column : column + width],
                start=(g == 0),
                stop=(g == THIRDS - 1),
            )

        def multiply(h, f):
            q = h // 2
            l, c = chunks[q]
            d = IRREP_DIMS[l]
            if l == 0:
                acc = banks.tile([P, 2 * P], F32, tag="bank")
                for g in range(THIRDS):
                    mx_pass(acc[:], 0, g, 0, h, 0, 2 * P)
                result = stream.tile([P, 2 * P], F32, name="result0", bufs=6)
                first = c * CHUNK + h % 2 * 2 * P
                late.append((result[:], acc[:], bias_rows[:, first : first + 2 * P]))
                results[h] = (first, result)
                done.append(h)
                return
            k, s = divmod(f, LINE)
            r, i = divmod(f, d)
            if f == 0:
                result = stream.tile([P, CHUNK * d], F32, name="result1" if l == 1 else "result", bufs=3 if l == 1 else 2)
                results[h + 1] = (SEGMENT_START[l] + c * CHUNK * d, result)
            if s == 0:
                acc = banks.tile([P, LINE, P], F32, tag="bank")
                sums[q] = acc
            acc = sums[q]
            for g in range(THIRDS):
                mx_pass(acc[:, s, :], l, g, i, h, r % 2 * P, P)
            if s == LINE - 1:
                lines = results[2 * q + 1][1][:].rearrange("p (j k s) -> p j k s", k=d, s=LINE)
                by_line = acc[:].rearrange("p s j -> p j s")
                if k % 2:
                    late.append((lines[:, :, k, :], by_line, None))
                else:
                    nc.scalar.copy(out=lines[:, :, k, :], in_=by_line)
            if f == 4 * d - 1:
                done.append(h)

        def drain_late():
            for target, source, addend in late:
                if addend is None:
                    nc.vector.tensor_copy(out=target, in_=source)
                else:
                    nc.vector.tensor_tensor(out=target, in0=source, in1=addend, op=mybir.AluOpType.add)
            late.clear()

        def store(h):
            first, result = results[h]
            width = result.shape[1]
            nc.scalar.dma_start(out=out[:, first : first + width], in_=result[:])

        for j in range(-LOAD, max(shares) + 1):
            if 0 <= j + LOAD < len(items):
                load(items[j + LOAD])
            if j + LOAD == len(items):
                nc.sync.dma_start(out=bias_rows[:], in_=bias.partition_broadcast(P))
            if 0 <= j - QUANT < len(items):
                quantize(items[j - QUANT])
            if 0 <= j + PREP < len(items):
                prepare(items[j + PREP])
            if 0 <= j < len(items):
                turn_item(items[j])
            for cell in shares.get(j, []):
                multiply(*cell)
            drain_late()
            for h in done:
                store(h)
            done.clear()
